import numpy as np
import ml_dtypes


def mxq(x, axis, fmt="e4m3"):
    dtype, down = {"e4m3": (ml_dtypes.float8_e4m3fn, 7), "e5m2": (ml_dtypes.float8_e5m2, 14)}[fmt]
    v = np.moveaxis(np.asarray(x, np.float32).astype(ml_dtypes.bfloat16).astype(np.float64), axis, -1)
    blocks = v.reshape(v.shape[:-1] + (-1, 32))
    amax = np.abs(blocks).max(-1, keepdims=True)
    byte = np.maximum(np.where(amax > 0, np.frexp(amax)[1] - 1 + 127, 0) - down, 1)
    scale = np.exp2(byte - 127.0)
    codes = (blocks / scale).astype(np.float32).astype(dtype).astype(np.float64)
    return np.moveaxis((codes * scale).reshape(v.shape), -1, axis)


WIDE = False


def mx_kscale(k):
    if not WIDE:
        return np.ones(k)
    levels = np.array([10, -10, 5, -5, 0])
    a = np.random.permutation(np.resize(levels, k // 512 * 4)).reshape(k // 512, 4)
    idx = np.arange(k)
    return np.exp2(a[idx // 512, idx % 128 // 32])


BF16 = ml_dtypes.bfloat16


def bf(x):
    return np.asarray(x, np.float32).astype(BF16)


def f64(x):
    return np.asarray(x).astype(np.float64)


B, N, D, H, L = 512, 4096, 512, 1024, 512


def setup_inputs():
    s = mx_kscale(H)
    return {"h": bf(np.tanh(np.random.standard_normal((B, H)) * 0.85) * s),
            "Wm": bf(np.random.standard_normal((H, L)) * 1.2 / np.sqrt(H) / s[:, None]),
            "bm": bf(np.random.standard_normal(L) * 0.2),
            "Wv": bf(np.random.standard_normal((H, L)) * 1.0 / np.sqrt(H) / s[:, None]),
            "bv": bf(-0.5 + np.random.standard_normal(L) * 0.2),
            "eps": bf(np.random.standard_normal((B, L))),
            "Wd1": bf(np.random.standard_normal((L, H)) * 0.8 / np.sqrt(L)),
            "bd1": bf(np.random.standard_normal(H) * 0.2)}


def reference(h, Wm, bm, Wv, bv, eps, Wd1, bd1):
    hq = mxq(f64(h), 1, "e4m3")
    z_mean = (hq @ mxq(f64(Wm), 0, "e4m3")) + f64(bm)
    z_log_var = (hq @ mxq(f64(Wv), 0, "e4m3")) + f64(bv)
    z = z_mean + np.exp(0.5 * z_log_var) * f64(eps)
    hd = np.tanh((mxq(z, 1, "e4m3") @ mxq(f64(Wd1), 0, "e4m3")) + f64(bd1))
    kl = -0.5 * np.mean(z_log_var - np.square(z_mean) - np.exp(z_log_var) + 1.0)
    return hd, np.reshape(kl, (1,))

@@ -1,0 +1,254 @@
+import concourse.mybir as mybir
+from concourse.masks import make_identity
+
+F32 = mybir.dt.float32
+BF16 = mybir.dt.bfloat16
+U32 = mybir.dt.uint32
+U8 = mybir.dt.uint8
+FP8X4 = mybir.dt.float8_e4m3fn_x4
+ACT = mybir.ActivationFunctionType
+ALU = mybir.AluOpType
+
+B, H, L = 512, 1024, 512
+P = 128
+PACK = 4
+K_PASS = P * PACK
+BANK = 512
+PSUM_BANKS = 8
+H_PASSES = H // K_PASS
+L_TILES = L // P
+B_TILES = B // P
+N_HALVES = H // BANK
+RUN = 4
+VECTOR_COLUMNS = 3 * BANK // 4
+
+FLOPS = 2 * B * H * L * 2 + 2 * B * L * H
+
+
+def tile_knowledgeawarevariationalautoencoder_pc_kernel(
+    tc, h, Wm, bm, Wv, bv, eps, Wd1, bd1, out_0, out_1
+):
+    nc = tc.nc
+    with tc.tile_pool(name="keep", bufs=1) as keep, tc.psum_pool(
+        name="psum", bufs=PSUM_BANKS
+    ) as psum, tc.manual_schedule():
+
+        def bank(shape, dtype, name):
+            return psum.tile(shape, dtype, name=name, tag="bank")
+
+        def regroup(raw, name):
+            grouped = keep.tile([P, BANK, PACK], BF16, name=name, align_bytes=64)
+            vector_part = slice(0, VECTOR_COLUMNS)
+            scalar_part = slice(VECTOR_COLUMNS, BANK)
+            nc.vector.tensor_copy(
+                out=grouped[:, vector_part, :].rearrange("p (c i) t -> p c t i", i=RUN),
+                in_=raw[:, :, vector_part].rearrange("p t (c i) -> p c t i", i=RUN),
+            )
+            nc.scalar.copy(
+                out=grouped[:, scalar_part, :].rearrange("p (c i) t -> p c t i", i=RUN),
+                in_=raw[:, :, scalar_part].rearrange("p t (c i) -> p c t i", i=RUN),
+            )
+            return grouped
+
+        def quantise(grouped, name):
+            codes = keep.tile([P, BANK], U32, name=name + "_codes", align_bytes=64)
+            scales = keep.tile([P, BANK], U8, name=name + "_scales", align_bytes=64)
+            nc.vector.quantize_mx(
+                out=codes[:].bitcast(FP8X4),
+                scales=scales[:],
+                in_=grouped[:].rearrange("p c t -> p (c t)"),
+            )
+            return codes, scales
+
+        def mx_pass(acc, stationary, columns, moving, start, stop):
+            nc.tensor.matmul_mx(
+                out=acc,
+                lhsT=stationary[0][:, columns].bitcast(FP8X4),
+                lhsT_scale=stationary[1][:, columns],
+                rhs=moving[0].bitcast(FP8X4),
+                rhs_scale=moving[1],
+                start=start,
+                stop=stop,
+            )
+
+        ident_f32 = keep.tile([P, P], F32, name="ident_f32")
+        make_identity(nc, ident_f32[:])
+        ident_bf16 = keep.tile([P, P], BF16, name="ident_bf16")
+        make_identity(nc, ident_bf16[:])
+        ones = keep.tile([P, P], F32, name="ones")
+        nc.vector.memset(ones[:], 1.0)
+        bias_rows = keep.tile([P, P], BF16, name="bias_rows")
+        nc.vector.memset(bias_rows[:], 0.0)
+
+        nc.scalar.dma_start(out=bias_rows[0:L_TILES, :], in_=bm.rearrange("(t p) -> t p", p=P))
+        nc.scalar.dma_start(out=bias_rows[L_TILES : 2 * L_TILES, :], in_=bv.rearrange("(t p) -> t p", p=P))
+
+        def load_first_weight(weight, g, name):
+            raw = keep.tile([P, PACK, L], BF16, name=name)
+            nc.sync.dma_start(
+                out=raw[:].rearrange("p (u e) c -> p u (e c)", u=2),
+                in_=weight[g * K_PASS : (g + 1) * K_PASS, :].rearrange("(u q e) c -> q u (e c)", u=2, e=2),
+            )
+            return raw
+
+        wv_raw = [load_first_weight(Wv, g, "wv_raw%d" % g) for g in range(H_PASSES)]
+        h_rows = []
+        for i in range(B_TILES):
+            h_tile = keep.tile([P, H], BF16, name="h_rows%d" % i)
+            nc.sync.dma_start(out=h_tile[:], in_=h[i * P : (i + 1) * P, :])
+            h_rows.append(h_tile)
+        eps_rows = keep.tile([P, B_TILES, L], BF16, name="eps_rows")
+        nc.sync.dma_start(out=eps_rows[:], in_=eps.rearrange("(i p) l -> p i l", p=P))
+        wm_raw = [load_first_weight(Wm, g, "wm_raw%d" % g) for g in range(H_PASSES)]
+        wd_raw = []
+        for j in range(N_HALVES):
+            wd_tile = keep.tile([P, PACK, BANK], BF16, name="wd_raw%d" % j)
+            nc.sync.dma_start(
+                out=wd_tile[:], in_=Wd1[:, j * BANK : (j + 1) * BANK].rearrange("(t p) n -> p t n", p=P)
+            )
+            wd_raw.append(wd_tile)
+        bd1_all = keep.tile([P, H], BF16, name="bd1_all")
+        nc.sync.dma_start(out=bd1_all[:], in_=bd1.partition_broadcast(P))
+
+        wv_grouped = [regroup(wv_raw[g], "wv_grouped%d" % g) for g in range(H_PASSES)]
+        wv_mx = [quantise(wv_grouped[g], "wv%d" % g) for g in range(H_PASSES)]
+
+        h_grouped = keep.tile([P, H_PASSES, B * PACK], BF16, name="h_grouped", align_bytes=64)
+        h_grouped_words = h_grouped[:].bitcast(F32).rearrange("p g (b u) -> p g b u", u=2)
+        for i in range(B_TILES):
+            h_bank = bank([P, H_PASSES, 2, P], F32, "h_bank%d" % i)
+            h_words = h_rows[i][:].bitcast(F32)
+            for g in range(H_PASSES):
+                for u in range(2):
+                    first_word = (2 * g + u) * P
+                    nc.tensor.transpose(h_bank[:, g, u, :], h_words[:, first_word : first_word + P], ident_f32[:])
+            nc.scalar.copy(
+                out=h_grouped_words[:, :, i * P : (i + 1) * P, :],
+                in_=h_bank[:].rearrange("p g u b -> p g b u"),
+            )
+        h_codes = keep.tile([P, H_PASSES, B], U32, name="h_codes", align_bytes=64)
+        h_scales = keep.tile([P, H_PASSES, B], U8, name="h_scales", align_bytes=64)
+        for g in range(H_PASSES):
+            nc.vector.quantize_mx(
+                out=h_codes[:, g, :].bitcast(FP8X4), scales=h_scales[:, g, :], in_=h_grouped[:, g, :]
+            )
+        h_mx = [(h_codes[:, g, :], h_scales[:, g, :]) for g in range(H_PASSES)]
+
+        bias_bank = bank([P, P], BF16, "bias_bank")
+        nc.tensor.transpose(bias_bank[:], bias_rows[:], ident_bf16[:])
+        bias_cols = keep.tile([P, 2 * L_TILES], F32, name="bias_cols")
+        nc.vector.tensor_copy(out=bias_cols[:], in_=bias_bank[:, 0 : 2 * L_TILES])
+        bm_cols = bias_cols[:, 0:L_TILES]
+        bv_cols = bias_cols[:, L_TILES : 2 * L_TILES]
+        half_bv_cols = keep.tile([P, L_TILES], F32, name="half_bv_cols")
+        nc.vector.tensor_scalar_mul(out=half_bv_cols[:], in0=bv_cols, scalar1=0.5)
+        minus_bv_cols = keep.tile([P, L_TILES], F32, name="minus_bv_cols")
+        nc.vector.tensor_scalar_mul(out=minus_bv_cols[:], in0=bv_cols, scalar1=-1.0)
+
+        def first_stage(weight_mx, name):
+            banks = []
+            for t in range(L_TILES):
+                acc = bank([P, B], F32, "%s%d" % (name, t))
+                for g in range(H_PASSES):
+                    mx_pass(
+                        acc[:], weight_mx[g], slice(t * P, (t + 1) * P), h_mx[g],
+                        start=(g == 0), stop=(g == H_PASSES - 1),
+                    )
+                banks.append(acc)
+            return banks
+
+        eps_banks = []
+        for pair in range(L_TILES // 2):
+            eps_bank = bank([P, 2, B], BF16, "eps_bank%d" % pair)
+            for s in range(2):
+                t = 2 * pair + s
+                for i in range(B_TILES):
+                    nc.tensor.transpose(
+                        eps_bank[:, s, i * P : (i + 1) * P], eps_rows[:, i, t * P : (t + 1) * P], ident_bf16[:]
+                    )
+            eps_banks.append(eps_bank)
+
+        zlv_banks = first_stage(wv_mx, "zlv_bank")
+
+        wm_grouped = [regroup(wm_raw[g], "wm_grouped%d" % g) for g in range(H_PASSES)]
+        wm_mx = [quantise(wm_grouped[g], "wm%d" % g) for g in range(H_PASSES)]
+
+        std = keep.tile([P, L_TILES, B], F32, name="std")
+        noise = keep.tile([P, L_TILES, B], F32, name="noise")
+        for t in range(L_TILES):
+            nc.scalar.activation(
+                out=std[:, t, :], in_=zlv_banks[t][:], func=ACT.Exp, bias=half_bv_cols[:, t : t + 1], scale=0.5
+            )
+        for t in range(L_TILES):
+            nc.vector.tensor_mul(out=noise[:, t, :], in0=std[:, t, :], in1=eps_banks[t // 2][:, t % 2, :])
+
+        zm_banks = first_stage(wm_mx, "zm_bank")
+
+        wd_grouped = [regroup(wd_raw[j], "wd_grouped%d" % j) for j in range(N_HALVES)]
+        wd_mx = [quantise(wd_grouped[j], "wd%d" % j) for j in range(N_HALVES)]
+
+        kl_sums = keep.tile([P, 2 * L_TILES + 1], F32, name="kl_sums")
+        unread = keep.tile([P, 3 * L_TILES, B], BF16, name="unread")
+        for t in range(L_TILES):
+            nc.scalar.activation(
+                out=unread[:, t, :], in_=zlv_banks[t][:], func=ACT.Identity, bias=minus_bv_cols[:, t : t + 1],
+                scale=-1.0, accum_out=kl_sums[:, t : t + 1],
+            )
+
+        z_rows = keep.tile([P, L_TILES, B], BF16, name="z_rows")
+        for t in range(L_TILES):
+            nc.vector.scalar_tensor_tensor(
+                out=z_rows[:, t, :], in0=zm_banks[t][:], scalar=bm_cols[:, t : t + 1], in1=noise[:, t, :],
+                op0=ALU.add, op1=ALU.add,
+            )
+            nc.scalar.activation(
+                out=unread[:, L_TILES + t, :], in_=zm_banks[t][:], func=ACT.Square, bias=bm_cols[:, t : t + 1],
+                accum_out=kl_sums[:, L_TILES + t : L_TILES + t + 1],
+            )
+
+        z_grouped = keep.tile([P, B, PACK], BF16, name="z_grouped", align_bytes=64)
+        z_codes = keep.tile([P, B], U32, name="z_codes", align_bytes=64)
+        z_scales = keep.tile([P, B], U8, name="z_scales", align_bytes=64)
+        halves = [slice(0, B // 2), slice(B // 2, B)]
+        for half in halves:
+            nc.vector.tensor_copy(
+                out=z_grouped[:, half, :].rearrange("p (c i) t -> p c t i", i=RUN),
+                in_=z_rows[:, :, half].rearrange("p t (c i) -> p c t i", i=RUN),
+            )
+        for half in halves:
+            nc.vector.quantize_mx(
+                out=z_codes[:, half].bitcast(FP8X4),
+                scales=z_scales[:, half],
+                in_=z_grouped[:, half, :].rearrange("p c t -> p (c t)"),
+            )
+        nc.scalar.activation(
+            out=unread[:, 2 * L_TILES : 3 * L_TILES, :], in_=std[:], func=ACT.Square,
+            accum_out=kl_sums[:, 2 * L_TILES : 2 * L_TILES + 1],
+        )
+
+        hd_banks = {}
+        for i in range(B_TILES):
+            for j in range(N_HALVES):
+                hd_banks[i, j] = bank([P, BANK], F32, "hd_bank%d_%d" % (i, j))
+                mx_pass(
+                    hd_banks[i, j][:], (z_codes, z_scales), slice(i * P, (i + 1) * P),
+                    (wd_mx[j][0][:], wd_mx[j][1][:]), start=True, stop=True,
+                )
+        kl_partial = keep.tile([P, 1], F32, name="kl_partial")
+        for i in range(B_TILES):
+            for j in range(N_HALVES):
+                columns = slice(j * BANK, (j + 1) * BANK)
+                hd = keep.tile([P, BANK], F32, name="hd%d_%d" % (i, j))
+                nc.vector.tensor_add(out=hd[:], in0=hd_banks[i, j][:], in1=bd1_all[:, columns])
+                nc.scalar.activation(out=hd[:], in_=hd[:], func=ACT.Tanh)
+                nc.sync.dma_start(out=out_0[i * P : (i + 1) * P, columns], in_=hd[:])
+            if i == B_TILES // 2 - 1:
+                nc.vector.tensor_reduce(out=kl_partial[:], in_=kl_sums[:], axis=mybir.AxisListType.X, op=ALU.add)
+                kl_bank = bank([P, 1], F32, "kl_bank")
+                nc.tensor.matmul(out=kl_bank[:], lhsT=ones[:], rhs=kl_partial[:], start=True, stop=True)
+
+        kl = keep.tile([P, 1], F32, name="kl")
+        nc.vector.tensor_scalar(
+            out=kl[:], in0=kl_bank[:], scalar1=0.5 / (B * L), scalar2=-0.5, op0=ALU.mult, op1=ALU.add
+        )
+        nc.sync.dma_start(out=out_1.rearrange("(a b) -> a b", a=1), in_=kl[0:1, :])

@@ -21,6 +21,7 @@ B_TILES = B // P
 N_HALVES = H // BANK
 RUN = 4
 VECTOR_COLUMNS = 3 * BANK // 4
+GPSIMD_COLUMNS = BANK // 2
 
 FLOPS = 2 * B * H * L * 2 + 2 * B * L * H
 
@@ -184,8 +185,16 @@ def tile_knowledgeawarevariationalautoencoder_pc_kernel(
 
         zm_banks = first_stage(wm_mx, "zm_bank")
 
-        wd_grouped = [regroup(wd_raw[j], "wd_grouped%d" % j) for j in range(N_HALVES)]
-        wd_mx = [quantise(wd_grouped[j], "wd%d" % j) for j in range(N_HALVES)]
+        wd_grouped = []
+        for j in range(N_HALVES):
+            grouped = keep.tile([P, BANK, PACK], BF16, name="wd_grouped%d" % j, align_bytes=64)
+            for first in range(0, BANK, GPSIMD_COLUMNS):
+                piece = slice(first, first + GPSIMD_COLUMNS)
+                nc.gpsimd.tensor_scalar(
+                    out=grouped[:, piece, :], in0=wd_raw[j][:, :, piece].rearrange("p t c -> p c t"),
+                    scalar1=1.0, scalar2=0.0, op0=ALU.mult, op1=ALU.add,
+                )
+            wd_grouped.append(grouped)
 
         kl_sums = keep.tile([P, 2 * L_TILES + 1], F32, name="kl_sums")
         unread = keep.tile([P, 3 * L_TILES, B], BF16, name="unread")
@@ -215,6 +224,7 @@ def tile_knowledgeawarevariationalautoencoder_pc_kernel(
                 out=z_grouped[:, half, :].rearrange("p (c i) t -> p c t i", i=RUN),
                 in_=z_rows[:, :, half].rearrange("p t (c i) -> p c t i", i=RUN),
             )
+        wd_mx = [quantise(wd_grouped[j], "wd%d" % j) for j in range(N_HALVES)]
         for half in halves:
             nc.vector.quantize_mx(
                 out=z_codes[:, half].bitcast(FP8X4),

@@ -20,7 +20,7 @@ L_TILES = L // P
 B_TILES = B // P
 N_HALVES = H // BANK
 RUN = 4
-VECTOR_COLUMNS = 3 * BANK // 4
+VECTOR_COLUMNS = 5 * BANK // 8
 GPSIMD_COLUMNS = BANK // 2
 
 FLOPS = 2 * B * H * L * 2 + 2 * B * L * H
@@ -98,9 +98,10 @@ def tile_knowledgeawarevariationalautoencoder_pc_kernel(
             h_tile = keep.tile([P, H], BF16, name="h_rows%d" % i)
             nc.sync.dma_start(out=h_tile[:], in_=h[i * P : (i + 1) * P, :])
             h_rows.append(h_tile)
+        wm_raw = [load_first_weight(Wm, 0, "wm_raw0")]
         eps_rows = keep.tile([P, B_TILES, L], BF16, name="eps_rows")
         nc.sync.dma_start(out=eps_rows[:], in_=eps.rearrange("(i p) l -> p i l", p=P))
-        wm_raw = [load_first_weight(Wm, g, "wm_raw%d" % g) for g in range(H_PASSES)]
+        wm_raw.append(load_first_weight(Wm, 1, "wm_raw1"))
         wd_raw = []
         for j in range(N_HALVES):
             wd_tile = keep.tile([P, PACK, BANK], BF16, name="wd_raw%d" % j)
@@ -127,6 +128,7 @@ def tile_knowledgeawarevariationalautoencoder_pc_kernel(
                 out=h_grouped_words[:, :, i * P : (i + 1) * P, :],
                 in_=h_bank[:].rearrange("p g u b -> p g b u"),
             )
+        wm_grouped = [regroup(wm_raw[0], "wm_grouped0")]
         h_codes = keep.tile([P, H_PASSES, B], U32, name="h_codes", align_bytes=64)
         h_scales = keep.tile([P, H_PASSES, B], U8, name="h_scales", align_bytes=64)
         for g in range(H_PASSES):
@@ -143,8 +145,10 @@ def tile_knowledgeawarevariationalautoencoder_pc_kernel(
         bv_cols = bias_cols[:, L_TILES : 2 * L_TILES]
         half_bv_cols = keep.tile([P, L_TILES], F32, name="half_bv_cols")
         nc.vector.tensor_scalar_mul(out=half_bv_cols[:], in0=bv_cols, scalar1=0.5)
-        minus_bv_cols = keep.tile([P, L_TILES], F32, name="minus_bv_cols")
-        nc.vector.tensor_scalar_mul(out=minus_bv_cols[:], in0=bv_cols, scalar1=-1.0)
+        bv_sum = keep.tile([P, 1], F32, name="bv_sum")
+        nc.vector.tensor_reduce(out=bv_sum[:], in_=bv_cols, axis=mybir.AxisListType.X, op=ALU.add)
+        minus_bv_share = keep.tile([P, 1], F32, name="minus_bv_share")
+        nc.vector.tensor_scalar_mul(out=minus_bv_share[:], in0=bv_sum[:], scalar1=-float(B // P))
 
         def first_stage(weight_mx, name):
             banks = []
@@ -171,7 +175,7 @@ def tile_knowledgeawarevariationalautoencoder_pc_kernel(
 
         zlv_banks = first_stage(wv_mx, "zlv_bank")
 
-        wm_grouped = [regroup(wm_raw[g], "wm_grouped%d" % g) for g in range(H_PASSES)]
+        wm_grouped.append(regroup(wm_raw[1], "wm_grouped1"))
         wm_mx = [quantise(wm_grouped[g], "wm%d" % g) for g in range(H_PASSES)]
 
         std = keep.tile([P, L_TILES, B], F32, name="std")
@@ -185,6 +189,15 @@ def tile_knowledgeawarevariationalautoencoder_pc_kernel(
 
         zm_banks = first_stage(wm_mx, "zm_bank")
 
+        zlv_total = bank([P, P], F32, "zlv_total")
+        total_passes = [(t, i, g) for t in range(L_TILES) for i in range(B_TILES) for g in range(H_PASSES)]
+        for t, i, g in total_passes:
+            b_cols = slice(i * P, (i + 1) * P)
+            mx_pass(
+                zlv_total[:], wv_mx[g], slice(t * P, (t + 1) * P), (h_codes[:, g, b_cols], h_scales[:, g, b_cols]),
+                start=((t, i, g) == total_passes[0]), stop=((t, i, g) == total_passes[-1]),
+            )
+
         wd_grouped = []
         for j in range(N_HALVES):
             grouped = keep.tile([P, BANK, PACK], BF16, name="wd_grouped%d" % j, align_bytes=64)
@@ -196,13 +209,8 @@ def tile_knowledgeawarevariationalautoencoder_pc_kernel(
                 )
             wd_grouped.append(grouped)
 
-        kl_sums = keep.tile([P, 2 * L_TILES + 1], F32, name="kl_sums")
-        unread = keep.tile([P, 3 * L_TILES, B], BF16, name="unread")
-        for t in range(L_TILES):
-            nc.scalar.activation(
-                out=unread[:, t, :], in_=zlv_banks[t][:], func=ACT.Identity, bias=minus_bv_cols[:, t : t + 1],
-                scale=-1.0, accum_out=kl_sums[:, t : t + 1],
-            )
+        kl_sums = keep.tile([P, L_TILES + 2], F32, name="kl_sums")
+        unread = keep.tile([P, 2 * L_TILES + 1, B], BF16, name="unread")
 
         z_rows = keep.tile([P, L_TILES, B], BF16, name="z_rows")
         for t in range(L_TILES):
@@ -211,19 +219,22 @@ def tile_knowledgeawarevariationalautoencoder_pc_kernel(
                 op0=ALU.add, op1=ALU.add,
             )
             nc.scalar.activation(
-                out=unread[:, L_TILES + t, :], in_=zm_banks[t][:], func=ACT.Square, bias=bm_cols[:, t : t + 1],
-                accum_out=kl_sums[:, L_TILES + t : L_TILES + t + 1],
+                out=unread[:, t, :], in_=zm_banks[t][:], func=ACT.Square, bias=bm_cols[:, t : t + 1],
+                accum_out=kl_sums[:, t : t + 1],
             )
 
         z_grouped = keep.tile([P, B, PACK], BF16, name="z_grouped", align_bytes=64)
         z_codes = keep.tile([P, B], U32, name="z_codes", align_bytes=64)
         z_scales = keep.tile([P, B], U8, name="z_scales", align_bytes=64)
         halves = [slice(0, B // 2), slice(B // 2, B)]
-        for half in halves:
-            nc.vector.tensor_copy(
-                out=z_grouped[:, half, :].rearrange("p (c i) t -> p c t i", i=RUN),
-                in_=z_rows[:, :, half].rearrange("p t (c i) -> p c t i", i=RUN),
-            )
+        nc.vector.tensor_copy(
+            out=z_grouped[:, halves[0], :].rearrange("p (c i) t -> p c t i", i=RUN),
+            in_=z_rows[:, :, halves[0]].rearrange("p t (c i) -> p c t i", i=RUN),
+        )
+        nc.scalar.copy(
+            out=z_grouped[:, halves[1], :].rearrange("p (c i) t -> p c t i", i=RUN),
+            in_=z_rows[:, :, halves[1]].rearrange("p t (c i) -> p c t i", i=RUN),
+        )
         wd_mx = [quantise(wd_grouped[j], "wd%d" % j) for j in range(N_HALVES)]
         for half in halves:
             nc.vector.quantize_mx(
@@ -232,8 +243,12 @@ def tile_knowledgeawarevariationalautoencoder_pc_kernel(
                 in_=z_grouped[:, half, :].rearrange("p c t -> p (c t)"),
             )
         nc.scalar.activation(
-            out=unread[:, 2 * L_TILES : 3 * L_TILES, :], in_=std[:], func=ACT.Square,
-            accum_out=kl_sums[:, 2 * L_TILES : 2 * L_TILES + 1],
+            out=unread[:, L_TILES, 0:P], in_=zlv_total[:], func=ACT.Identity, bias=minus_bv_share[:], scale=-1.0,
+            accum_out=kl_sums[:, L_TILES : L_TILES + 1],
+        )
+        nc.scalar.activation(
+            out=unread[:, L_TILES + 1 : 2 * L_TILES + 1, :], in_=std[:], func=ACT.Square,
+            accum_out=kl_sums[:, L_TILES + 1 : L_TILES + 2],
         )
 
         hd_banks = {}

@@ -184,6 +184,12 @@ def tile_knowledgeawarevariationalautoencoder_pc_kernel(
             nc.scalar.activation(
                 out=std[:, t, :], in_=zlv_banks[t][:], func=ACT.Exp, bias=half_bv_cols[:, t : t + 1], scale=0.5
             )
+        kl_sums = keep.tile([P, L_TILES + 2], F32, name="kl_sums")
+        unread = keep.tile([P, 2 * L_TILES + 1, B], BF16, name="unread")
+        nc.scalar.activation(
+            out=unread[:, L_TILES + 1 : 2 * L_TILES + 1, :], in_=std[:], func=ACT.Square,
+            accum_out=kl_sums[:, L_TILES + 1 : L_TILES + 2],
+        )
         for t in range(L_TILES):
             nc.vector.tensor_mul(out=noise[:, t, :], in0=std[:, t, :], in1=eps_banks[t // 2][:, t % 2, :])
 
@@ -209,8 +215,6 @@ def tile_knowledgeawarevariationalautoencoder_pc_kernel(
                 )
             wd_grouped.append(grouped)
 
-        kl_sums = keep.tile([P, L_TILES + 2], F32, name="kl_sums")
-        unread = keep.tile([P, 2 * L_TILES + 1, B], BF16, name="unread")
 
         z_rows = keep.tile([P, L_TILES, B], BF16, name="z_rows")
         for t in range(L_TILES):
@@ -245,10 +249,6 @@ def tile_knowledgeawarevariationalautoencoder_pc_kernel(
         nc.scalar.activation(
             out=unread[:, L_TILES, 0:P], in_=zlv_total[:], func=ACT.Identity, bias=minus_bv_share[:], scale=-1.0,
             accum_out=kl_sums[:, L_TILES : L_TILES + 1],
-        )
-        nc.scalar.activation(
-            out=unread[:, L_TILES + 1 : 2 * L_TILES + 1, :], in_=std[:], func=ACT.Square,
-            accum_out=kl_sums[:, L_TILES + 1 : L_TILES + 2],
         )
 
         hd_banks = {}

@@ -80,9 +80,14 @@ def tile_knowledgeawarevariationalautoencoder_pc_kernel(
         nc.vector.memset(ones[:], 1.0)
         bias_rows = keep.tile([P, P], BF16, name="bias_rows")
         nc.vector.memset(bias_rows[:], 0.0)
+        ones_bf16 = keep.tile([P, P], BF16, name="ones_bf16")
+        nc.vector.memset(ones_bf16[:], 1.0)
+        bd1_row = keep.tile([P, H], BF16, name="bd1_row")
+        nc.vector.memset(bd1_row[:], 0.0)
 
         nc.scalar.dma_start(out=bias_rows[0:L_TILES, :], in_=bm.rearrange("(t p) -> t p", p=P))
         nc.scalar.dma_start(out=bias_rows[L_TILES : 2 * L_TILES, :], in_=bv.rearrange("(t p) -> t p", p=P))
+        nc.scalar.dma_start(out=bd1_row[0:1, :], in_=bd1.rearrange("(a n) -> a n", a=1))
 
         def load_first_weight(weight, g, name):
             raw = keep.tile([P, PACK, L], BF16, name=name)
@@ -109,8 +114,14 @@ def tile_knowledgeawarevariationalautoencoder_pc_kernel(
                 out=wd_tile[:], in_=Wd1[:, j * BANK : (j + 1) * BANK].rearrange("(t p) n -> p t n", p=P)
             )
             wd_raw.append(wd_tile)
-        bd1_all = keep.tile([P, H], BF16, name="bd1_all")
-        nc.sync.dma_start(out=bd1_all[:], in_=bd1.partition_broadcast(P))
+
+        bd1_banks = []
+        for j in range(N_HALVES):
+            bd1_bank = bank([P, BANK], F32, "bd1_bank%d" % j)
+            nc.tensor.matmul(
+                out=bd1_bank[:], lhsT=ones_bf16[:], rhs=bd1_row[:, j * BANK : (j + 1) * BANK], start=True, stop=True
+            )
+            bd1_banks.append(bd1_bank)
 
         wv_grouped = [regroup(wv_raw[g], "wv_grouped%d" % g) for g in range(H_PASSES)]
         wv_mx = [quantise(wv_grouped[g], "wv%d" % g) for g in range(H_PASSES)]
@@ -129,6 +140,9 @@ def tile_knowledgeawarevariationalautoencoder_pc_kernel(
                 in_=h_bank[:].rearrange("p g u b -> p g b u"),
             )
         wm_grouped = [regroup(wm_raw[0], "wm_grouped0")]
+        bd1_all = keep.tile([P, H], BF16, name="bd1_all")
+        for j in range(N_HALVES):
+            nc.scalar.copy(out=bd1_all[:, j * BANK : (j + 1) * BANK], in_=bd1_banks[j][:])
         h_codes = keep.tile([P, H_PASSES, B], U32, name="h_codes", align_bytes=64)
         h_scales = keep.tile([P, H_PASSES, B], U8, name="h_scales", align_bytes=64)
         for g in range(H_PASSES):

@@ -83,11 +83,11 @@ def tile_knowledgeawarevariationalautoencoder_pc_kernel(
         ones_bf16 = keep.tile([P, P], BF16, name="ones_bf16")
         nc.vector.memset(ones_bf16[:], 1.0)
         bd1_row = keep.tile([P, H], BF16, name="bd1_row")
-        nc.vector.memset(bd1_row[:], 0.0)
+        nc.gpsimd.memset(bd1_row[:], 0.0)
+        nc.gpsimd.dma_start(out=bd1_row[0:1, :], in_=bd1.rearrange("(a n) -> a n", a=1))
 
         nc.scalar.dma_start(out=bias_rows[0:L_TILES, :], in_=bm.rearrange("(t p) -> t p", p=P))
         nc.scalar.dma_start(out=bias_rows[L_TILES : 2 * L_TILES, :], in_=bv.rearrange("(t p) -> t p", p=P))
-        nc.scalar.dma_start(out=bd1_row[0:1, :], in_=bd1.rearrange("(a n) -> a n", a=1))
 
         def load_first_weight(weight, g, name):
             raw = keep.tile([P, PACK, L], BF16, name=name)
@@ -115,14 +115,6 @@ def tile_knowledgeawarevariationalautoencoder_pc_kernel(
             )
             wd_raw.append(wd_tile)
 
-        bd1_banks = []
-        for j in range(N_HALVES):
-            bd1_bank = bank([P, BANK], F32, "bd1_bank%d" % j)
-            nc.tensor.matmul(
-                out=bd1_bank[:], lhsT=ones_bf16[:], rhs=bd1_row[:, j * BANK : (j + 1) * BANK], start=True, stop=True
-            )
-            bd1_banks.append(bd1_bank)
-
         wv_grouped = [regroup(wv_raw[g], "wv_grouped%d" % g) for g in range(H_PASSES)]
         wv_mx = [quantise(wv_grouped[g], "wv%d" % g) for g in range(H_PASSES)]
 
@@ -140,9 +132,6 @@ def tile_knowledgeawarevariationalautoencoder_pc_kernel(
                 in_=h_bank[:].rearrange("p g u b -> p g b u"),
             )
         wm_grouped = [regroup(wm_raw[0], "wm_grouped0")]
-        bd1_all = keep.tile([P, H], BF16, name="bd1_all")
-        for j in range(N_HALVES):
-            nc.scalar.copy(out=bd1_all[:, j * BANK : (j + 1) * BANK], in_=bd1_banks[j][:])
         h_codes = keep.tile([P, H_PASSES, B], U32, name="h_codes", align_bytes=64)
         h_scales = keep.tile([P, H_PASSES, B], U8, name="h_scales", align_bytes=64)
         for g in range(H_PASSES):
@@ -153,6 +142,17 @@ def tile_knowledgeawarevariationalautoencoder_pc_kernel(
 
         bias_bank = bank([P, P], BF16, "bias_bank")
         nc.tensor.transpose(bias_bank[:], bias_rows[:], ident_bf16[:])
+
+        bd1_banks = []
+        for j in range(N_HALVES):
+            bd1_bank = bank([P, BANK], F32, "bd1_bank%d" % j)
+            nc.tensor.matmul(
+                out=bd1_bank[:], lhsT=ones_bf16[:], rhs=bd1_row[:, j * BANK : (j + 1) * BANK], start=True, stop=True
+            )
+            bd1_banks.append(bd1_bank)
+        bd1_all = keep.tile([P, H], BF16, name="bd1_all")
+        for j in range(N_HALVES):
+            nc.scalar.copy(out=bd1_all[:, j * BANK : (j + 1) * BANK], in_=bd1_banks[j][:])
         bias_cols = keep.tile([P, 2 * L_TILES], F32, name="bias_cols")
         nc.vector.tensor_copy(out=bias_cols[:], in_=bias_bank[:, 0 : 2 * L_TILES])
         bm_cols = bias_cols[:, 0:L_TILES]

@@ -253,7 +253,7 @@ def tile_knowledgeawarevariationalautoencoder_pc_kernel(
             out=z_grouped[:, halves[1], :].rearrange("p (c i) t -> p c t i", i=RUN),
             in_=z_rows[:, :, halves[1]].rearrange("p t (c i) -> p c t i", i=RUN),
         )
-        wd_mx = [quantise(wd_grouped[j], "wd%d" % j) for j in range(N_HALVES)]
+        wd_mx = [quantise(wd_grouped[0], "wd0")]
         for half in halves:
             nc.vector.quantize_mx(
                 out=z_codes[:, half].bitcast(FP8X4),
@@ -266,25 +266,35 @@ def tile_knowledgeawarevariationalautoencoder_pc_kernel(
         )
 
         hd_banks = {}
-        for i in range(B_TILES):
-            for j in range(N_HALVES):
+
+        def second_stage_passes(j):
+            for i in range(B_TILES):
                 hd_banks[i, j] = bank([P, BANK], F32, "hd_bank%d_%d" % (i, j))
                 mx_pass(
                     hd_banks[i, j][:], (z_codes, z_scales), slice(i * P, (i + 1) * P),
                     (wd_mx[j][0][:], wd_mx[j][1][:]), start=True, stop=True,
                 )
+
+        def finish(i, j):
+            columns = slice(j * BANK, (j + 1) * BANK)
+            hd = keep.tile([P, BANK], F32, name="hd%d_%d" % (i, j))
+            nc.vector.tensor_add(out=hd[:], in0=hd_banks[i, j][:], in1=bd1_all[:, columns])
+            nc.scalar.activation(out=hd[:], in_=hd[:], func=ACT.Tanh)
+            nc.sync.dma_start(out=out_0[i * P : (i + 1) * P, columns], in_=hd[:])
+
+        second_stage_passes(0)
+        finish(0, 0)
+        finish(1, 0)
+        wd_mx.append(quantise(wd_grouped[1], "wd1"))
+        second_stage_passes(1)
+        finish(2, 0)
+        finish(3, 0)
         kl_partial = keep.tile([P, 1], F32, name="kl_partial")
+        nc.vector.tensor_reduce(out=kl_partial[:], in_=kl_sums[:], axis=mybir.AxisListType.X, op=ALU.add)
+        kl_bank = bank([P, 1], F32, "kl_bank")
+        nc.tensor.matmul(out=kl_bank[:], lhsT=ones[:], rhs=kl_partial[:], start=True, stop=True)
         for i in range(B_TILES):
-            for j in range(N_HALVES):
-                columns = slice(j * BANK, (j + 1) * BANK)
-                hd = keep.tile([P, BANK], F32, name="hd%d_%d" % (i, j))
-                nc.vector.tensor_add(out=hd[:], in0=hd_banks[i, j][:], in1=bd1_all[:, columns])
-                nc.scalar.activation(out=hd[:], in_=hd[:], func=ACT.Tanh)
-                nc.sync.dma_start(out=out_0[i * P : (i + 1) * P, columns], in_=hd[:])
-            if i == B_TILES // 2 - 1:
-                nc.vector.tensor_reduce(out=kl_partial[:], in_=kl_sums[:], axis=mybir.AxisListType.X, op=ALU.add)
-                kl_bank = bank([P, 1], F32, "kl_bank")
-                nc.tensor.matmul(out=kl_bank[:], lhsT=ones[:], rhs=kl_partial[:], start=True, stop=True)
+            finish(i, 1)
 
         kl = keep.tile([P, 1], F32, name="kl")
         nc.vector.tensor_scalar(

import concourse.mybir as mybir
from concourse.masks import make_identity

F32 = mybir.dt.float32
BF16 = mybir.dt.bfloat16
U32 = mybir.dt.uint32
U8 = mybir.dt.uint8
FP8X4 = mybir.dt.float8_e4m3fn_x4
ACT = mybir.ActivationFunctionType
ALU = mybir.AluOpType

B, H, L = 512, 1024, 512
P = 128
PACK = 4
K_PASS = P * PACK
BANK = 512
PSUM_BANKS = 8
H_PASSES = H // K_PASS
L_TILES = L // P
B_TILES = B // P
N_HALVES = H // BANK
RUN = 4
VECTOR_COLUMNS = 5 * BANK // 8
GPSIMD_COLUMNS = BANK // 2

FLOPS = 2 * B * H * L * 2 + 2 * B * L * H


def tile_knowledgeawarevariationalautoencoder_pc_kernel(
    tc, h, Wm, bm, Wv, bv, eps, Wd1, bd1, out_0, out_1
):
    nc = tc.nc
    with tc.tile_pool(name="keep", bufs=1) as keep, tc.psum_pool(
        name="psum", bufs=PSUM_BANKS
    ) as psum, tc.manual_schedule():

        def bank(shape, dtype, name):
            return psum.tile(shape, dtype, name=name, tag="bank")

        def regroup(raw, name):
            grouped = keep.tile([P, BANK, PACK], BF16, name=name, align_bytes=64)
            vector_part = slice(0, VECTOR_COLUMNS)
            scalar_part = slice(VECTOR_COLUMNS, BANK)
            nc.vector.tensor_copy(
                out=grouped[:, vector_part, :].rearrange("p (c i) t -> p c t i", i=RUN),
                in_=raw[:, :, vector_part].rearrange("p t (c i) -> p c t i", i=RUN),
            )
            nc.scalar.copy(
                out=grouped[:, scalar_part, :].rearrange("p (c i) t -> p c t i", i=RUN),
                in_=raw[:, :, scalar_part].rearrange("p t (c i) -> p c t i", i=RUN),
            )
            return grouped

        def quantise(grouped, name):
            codes = keep.tile([P, BANK], U32, name=name + "_codes", align_bytes=64)
            scales = keep.tile([P, BANK], U8, name=name + "_scales", align_bytes=64)
            nc.vector.quantize_mx(
                out=codes[:].bitcast(FP8X4),
                scales=scales[:],
                in_=grouped[:].rearrange("p c t -> p (c t)"),
            )
            return codes, scales

        def mx_pass(acc, stationary, columns, moving, start, stop):
            nc.tensor.matmul_mx(
                out=acc,
                lhsT=stationary[0][:, columns].bitcast(FP8X4),
                lhsT_scale=stationary[1][:, columns],
                rhs=moving[0].bitcast(FP8X4),
                rhs_scale=moving[1],
                start=start,
                stop=stop,
            )

        ident_f32 = keep.tile([P, P], F32, name="ident_f32")
        make_identity(nc, ident_f32[:])
        ident_bf16 = keep.tile([P, P], BF16, name="ident_bf16")
        make_identity(nc, ident_bf16[:])
        ones = keep.tile([P, P], F32, name="ones")
        nc.vector.memset(ones[:], 1.0)
        bias_rows = keep.tile([P, P], BF16, name="bias_rows")
        nc.vector.memset(bias_rows[:], 0.0)
        ones_bf16 = keep.tile([P, P], BF16, name="ones_bf16")
        nc.vector.memset(ones_bf16[:], 1.0)
        bd1_row = keep.tile([P, H], BF16, name="bd1_row")
        nc.gpsimd.memset(bd1_row[:], 0.0)
        nc.gpsimd.dma_start(out=bd1_row[0:1, :], in_=bd1.rearrange("(a n) -> a n", a=1))

        nc.scalar.dma_start(out=bias_rows[0:L_TILES, :], in_=bm.rearrange("(t p) -> t p", p=P))
        nc.scalar.dma_start(out=bias_rows[L_TILES : 2 * L_TILES, :], in_=bv.rearrange("(t p) -> t p", p=P))

        def load_first_weight(weight, g, name):
            raw = keep.tile([P, PACK, L], BF16, name=name)
            nc.sync.dma_start(
                out=raw[:].rearrange("p (u e) c -> p u (e c)", u=2),
                in_=weight[g * K_PASS : (g + 1) * K_PASS, :].rearrange("(u q e) c -> q u (e c)", u=2, e=2),
            )
            return raw

        wv_raw = [load_first_weight(Wv, g, "wv_raw%d" % g) for g in range(H_PASSES)]
        h_rows = []
        for i in range(B_TILES):
            h_tile = keep.tile([P, H], BF16, name="h_rows%d" % i)
            nc.sync.dma_start(out=h_tile[:], in_=h[i * P : (i + 1) * P, :])
            h_rows.append(h_tile)
        wm_raw = [load_first_weight(Wm, 0, "wm_raw0")]
        eps_rows = keep.tile([P, B_TILES, L], BF16, name="eps_rows")
        nc.sync.dma_start(out=eps_rows[:], in_=eps.rearrange("(i p) l -> p i l", p=P))
        wm_raw.append(load_first_weight(Wm, 1, "wm_raw1"))
        wd_raw = []
        for j in range(N_HALVES):
            wd_tile = keep.tile([P, PACK, BANK], BF16, name="wd_raw%d" % j)
            nc.sync.dma_start(
                out=wd_tile[:], in_=Wd1[:, j * BANK : (j + 1) * BANK].rearrange("(t p) n -> p t n", p=P)
            )
            wd_raw.append(wd_tile)

        wv_grouped = [regroup(wv_raw[g], "wv_grouped%d" % g) for g in range(H_PASSES)]
        wv_mx = [quantise(wv_grouped[g], "wv%d" % g) for g in range(H_PASSES)]

        h_grouped = keep.tile([P, H_PASSES, B * PACK], BF16, name="h_grouped", align_bytes=64)
        h_grouped_words = h_grouped[:].bitcast(F32).rearrange("p g (b u) -> p g b u", u=2)
        for i in range(B_TILES):
            h_bank = bank([P, H_PASSES, 2, P], F32, "h_bank%d" % i)
            h_words = h_rows[i][:].bitcast(F32)
            for g in range(H_PASSES):
                for u in range(2):
                    first_word = (2 * g + u) * P
                    nc.tensor.transpose(h_bank[:, g, u, :], h_words[:, first_word : first_word + P], ident_f32[:])
            nc.scalar.copy(
                out=h_grouped_words[:, :, i * P : (i + 1) * P, :],
                in_=h_bank[:].rearrange("p g u b -> p g b u"),
            )
        wm_grouped = [regroup(wm_raw[0], "wm_grouped0")]
        h_codes = keep.tile([P, H_PASSES, B], U32, name="h_codes", align_bytes=64)
        h_scales = keep.tile([P, H_PASSES, B], U8, name="h_scales", align_bytes=64)
        for g in range(H_PASSES):
            nc.vector.quantize_mx(
                out=h_codes[:, g, :].bitcast(FP8X4), scales=h_scales[:, g, :], in_=h_grouped[:, g, :]
            )
        h_mx = [(h_codes[:, g, :], h_scales[:, g, :]) for g in range(H_PASSES)]

        bias_bank = bank([P, P], BF16, "bias_bank")
        nc.tensor.transpose(bias_bank[:], bias_rows[:], ident_bf16[:])

        bd1_banks = []
        for j in range(N_HALVES):
            bd1_bank = bank([P, BANK], F32, "bd1_bank%d" % j)
            nc.tensor.matmul(
                out=bd1_bank[:], lhsT=ones_bf16[:], rhs=bd1_row[:, j * BANK : (j + 1) * BANK], start=True, stop=True
            )
            bd1_banks.append(bd1_bank)
        bd1_all = keep.tile([P, H], BF16, name="bd1_all")
        for j in range(N_HALVES):
            nc.scalar.copy(out=bd1_all[:, j * BANK : (j + 1) * BANK], in_=bd1_banks[j][:])
        bias_cols = keep.tile([P, 2 * L_TILES], F32, name="bias_cols")
        nc.vector.tensor_copy(out=bias_cols[:], in_=bias_bank[:, 0 : 2 * L_TILES])
        bm_cols = bias_cols[:, 0:L_TILES]
        bv_cols = bias_cols[:, L_TILES : 2 * L_TILES]
        half_bv_cols = keep.tile([P, L_TILES], F32, name="half_bv_cols")
        nc.vector.tensor_scalar_mul(out=half_bv_cols[:], in0=bv_cols, scalar1=0.5)
        bv_sum = keep.tile([P, 1], F32, name="bv_sum")
        nc.vector.tensor_reduce(out=bv_sum[:], in_=bv_cols, axis=mybir.AxisListType.X, op=ALU.add)
        minus_bv_share = keep.tile([P, 1], F32, name="minus_bv_share")
        nc.vector.tensor_scalar_mul(out=minus_bv_share[:], in0=bv_sum[:], scalar1=-float(B // P))

        def first_stage(weight_mx, name):
            banks = []
            for t in range(L_TILES):
                acc = bank([P, B], F32, "%s%d" % (name, t))
                for g in range(H_PASSES):
                    mx_pass(
                        acc[:], weight_mx[g], slice(t * P, (t + 1) * P), h_mx[g],
                        start=(g == 0), stop=(g == H_PASSES - 1),
                    )
                banks.append(acc)
            return banks

        eps_banks = []
        for pair in range(L_TILES // 2):
            eps_bank = bank([P, 2, B], BF16, "eps_bank%d" % pair)
            for s in range(2):
                t = 2 * pair + s
                for i in range(B_TILES):
                    nc.tensor.transpose(
                        eps_bank[:, s, i * P : (i + 1) * P], eps_rows[:, i, t * P : (t + 1) * P], ident_bf16[:]
                    )
            eps_banks.append(eps_bank)

        zlv_banks = first_stage(wv_mx, "zlv_bank")

        wm_grouped.append(regroup(wm_raw[1], "wm_grouped1"))
        wm_mx = [quantise(wm_grouped[g], "wm%d" % g) for g in range(H_PASSES)]

        std = keep.tile([P, L_TILES, B], F32, name="std")
        noise = keep.tile([P, L_TILES, B], F32, name="noise")
        for t in range(L_TILES):
            nc.scalar.activation(
                out=std[:, t, :], in_=zlv_banks[t][:], func=ACT.Exp, bias=half_bv_cols[:, t : t + 1], scale=0.5
            )
        kl_sums = keep.tile([P, L_TILES + 2], F32, name="kl_sums")
        unread = keep.tile([P, 2 * L_TILES + 1, B], BF16, name="unread")
        nc.scalar.activation(
            out=unread[:, L_TILES + 1 : 2 * L_TILES + 1, :], in_=std[:], func=ACT.Square,
            accum_out=kl_sums[:, L_TILES + 1 : L_TILES + 2],
        )
        for t in range(L_TILES):
            nc.vector.tensor_mul(out=noise[:, t, :], in0=std[:, t, :], in1=eps_banks[t // 2][:, t % 2, :])

        zm_banks = first_stage(wm_mx, "zm_bank")

        zlv_total = bank([P, P], F32, "zlv_total")
        total_passes = [(t, i, g) for t in range(L_TILES) for i in range(B_TILES) for g in range(H_PASSES)]
        for t, i, g in total_passes:
            b_cols = slice(i * P, (i + 1) * P)
            mx_pass(
                zlv_total[:], wv_mx[g], slice(t * P, (t + 1) * P), (h_codes[:, g, b_cols], h_scales[:, g, b_cols]),
                start=((t, i, g) == total_passes[0]), stop=((t, i, g) == total_passes[-1]),
            )

        wd_grouped = []
        for j in range(N_HALVES):
            grouped = keep.tile([P, BANK, PACK], BF16, name="wd_grouped%d" % j, align_bytes=64)
            for first in range(0, BANK, GPSIMD_COLUMNS):
                piece = slice(first, first + GPSIMD_COLUMNS)
                nc.gpsimd.tensor_scalar(
                    out=grouped[:, piece, :], in0=wd_raw[j][:, :, piece].rearrange("p t c -> p c t"),
                    scalar1=1.0, scalar2=0.0, op0=ALU.mult, op1=ALU.add,
                )
            wd_grouped.append(grouped)


        z_rows = keep.tile([P, L_TILES, B], BF16, name="z_rows")
        for t in range(L_TILES):
            nc.vector.scalar_tensor_tensor(
                out=z_rows[:, t, :], in0=zm_banks[t][:], scalar=bm_cols[:, t : t + 1], in1=noise[:, t, :],
                op0=ALU.add, op1=ALU.add,
            )
            nc.scalar.activation(
                out=unread[:, t, :], in_=zm_banks[t][:], func=ACT.Square, bias=bm_cols[:, t : t + 1],
                accum_out=kl_sums[:, t : t + 1],
            )

        z_grouped = keep.tile([P, B, PACK], BF16, name="z_grouped", align_bytes=64)
        z_codes = keep.tile([P, B], U32, name="z_codes", align_bytes=64)
        z_scales = keep.tile([P, B], U8, name="z_scales", align_bytes=64)
        halves = [slice(0, B // 2), slice(B // 2, B)]
        nc.vector.tensor_copy(
            out=z_grouped[:, halves[0], :].rearrange("p (c i) t -> p c t i", i=RUN),
            in_=z_rows[:, :, halves[0]].rearrange("p t (c i) -> p c t i", i=RUN),
        )
        nc.scalar.copy(
            out=z_grouped[:, halves[1], :].rearrange("p (c i) t -> p c t i", i=RUN),
            in_=z_rows[:, :, halves[1]].rearrange("p t (c i) -> p c t i", i=RUN),
        )
        wd_mx = [quantise(wd_grouped[0], "wd0")]
        for half in halves:
            nc.vector.quantize_mx(
                out=z_codes[:, half].bitcast(FP8X4),
                scales=z_scales[:, half],
                in_=z_grouped[:, half, :].rearrange("p c t -> p (c t)"),
            )
        nc.scalar.activation(
            out=unread[:, L_TILES, 0:P], in_=zlv_total[:], func=ACT.Identity, bias=minus_bv_share[:], scale=-1.0,
            accum_out=kl_sums[:, L_TILES : L_TILES + 1],
        )

        hd_banks = {}

        def second_stage_passes(j):
            for i in range(B_TILES):
                hd_banks[i, j] = bank([P, BANK], F32, "hd_bank%d_%d" % (i, j))
                mx_pass(
                    hd_banks[i, j][:], (z_codes, z_scales), slice(i * P, (i + 1) * P),
                    (wd_mx[j][0][:], wd_mx[j][1][:]), start=True, stop=True,
                )

        def finish(i, j):
            columns = slice(j * BANK, (j + 1) * BANK)
            hd = keep.tile([P, BANK], F32, name="hd%d_%d" % (i, j))
            nc.vector.tensor_add(out=hd[:], in0=hd_banks[i, j][:], in1=bd1_all[:, columns])
            nc.scalar.activation(out=hd[:], in_=hd[:], func=ACT.Tanh)
            nc.sync.dma_start(out=out_0[i * P : (i + 1) * P, columns], in_=hd[:])

        second_stage_passes(0)
        finish(0, 0)
        finish(1, 0)
        wd_mx.append(quantise(wd_grouped[1], "wd1"))
        second_stage_passes(1)
        finish(2, 0)
        finish(3, 0)
        kl_partial = keep.tile([P, 1], F32, name="kl_partial")
        nc.vector.tensor_reduce(out=kl_partial[:], in_=kl_sums[:], axis=mybir.AxisListType.X, op=ALU.add)
        kl_bank = bank([P, 1], F32, "kl_bank")
        nc.tensor.matmul(out=kl_bank[:], lhsT=ones[:], rhs=kl_partial[:], start=True, stop=True)
        for i in range(B_TILES):
            finish(i, 1)

        kl = keep.tile([P, 1], F32, name="kl")
        nc.vector.tensor_scalar(
            out=kl[:], in0=kl_bank[:], scalar1=0.5 / (B * L), scalar2=-0.5, op0=ALU.mult, op1=ALU.add
        )
        nc.sync.dma_start(out=out_1.rearrange("(a b) -> a b", a=1), in_=kl[0:1, :])
